import numpy as np
import ml_dtypes


def mxq(x, axis, fmt="e4m3"):
    dtype, down = {"e4m3": (ml_dtypes.float8_e4m3fn, 7), "e5m2": (ml_dtypes.float8_e5m2, 14)}[fmt]
    v = np.moveaxis(np.asarray(x, np.float32).astype(ml_dtypes.bfloat16).astype(np.float64), axis, -1)
    blocks = v.reshape(v.shape[:-1] + (-1, 32))
    amax = np.abs(blocks).max(-1, keepdims=True)
    byte = np.maximum(np.where(amax > 0, np.frexp(amax)[1] - 1 + 127, 0) - down, 1)
    scale = np.exp2(byte - 127.0)
    codes = (blocks / scale).astype(np.float32).astype(dtype).astype(np.float64)
    return np.moveaxis((codes * scale).reshape(v.shape), -1, axis)


WIDE = False


def mx_kscale(k):
    if not WIDE:
        return np.ones(k)
    levels = np.array([10, -10, 5, -5, 0])
    if k % 512:
        return np.exp2(np.random.permutation(np.resize(levels, k // 32))).repeat(32)
    a = np.empty((k // 512, 16))
    for p in range(k // 512):
        a[p, :8] = np.random.permutation(np.resize(levels, 8))
        for g in range(8):
            far = levels[np.abs(levels - a[p, g]) >= 10]
            a[p, g + 8] = far[np.random.randint(len(far))]
    return np.exp2(a.ravel()).repeat(32)


BF16 = ml_dtypes.bfloat16


def bf(x):
    return np.asarray(x, np.float32).astype(BF16)


def f64(x):
    return np.asarray(x).astype(np.float64)


M, K, N = 1024, 1024, 2048
BLOCK = 128


def block_scales(weight_scale_inv, n, k):
    nb, kb = weight_scale_inv.shape
    return np.broadcast_to(f64(weight_scale_inv)[:, None, :, None], (nb, BLOCK, kb, BLOCK)).reshape(n, k)


def setup_inputs():
    s = mx_kscale(M)[:, None]
    u = mx_kscale(N)
    x0 = bf(np.random.standard_normal((M, K)))
    weight0 = bf(np.random.standard_normal((N, K)) / np.sqrt(K))
    weight_scale_inv = bf(np.random.uniform(0.5, 1.5, (N // BLOCK, K // BLOCK)))
    bias = bf(np.random.standard_normal(N) * 0.3)
    g = bf(np.random.standard_normal((M, N)) * np.exp2(np.random.randint(-6, 1, (M, 1))) / s * u[None, :])
    return {"x": bf(f64(x0) * s),
            "weight": bf(f64(weight0) / u[:, None]),
            "weight_scale_inv": weight_scale_inv,
            "bias": bias,
            "grad_out": g}


def reference(x, weight, weight_scale_inv, bias, grad_out):
    n, k = weight.shape
    sc = block_scales(weight_scale_inv, n, k)
    w_deq = f64(weight) * sc
    g = f64(grad_out)
    dx = mxq(g, 1, "e5m2") @ mxq(w_deq, 0, "e4m3")
    dw_deq = mxq(g, 0, "e5m2").T @ mxq(f64(x), 0, "e4m3")
    return dx, dw_deq * sc

@@ -1,0 +1,323 @@
+from contextlib import ExitStack
+
+import concourse.mybir as mybir
+from concourse.masks import make_identity
+
+TOKENS, K, N = 1024, 1024, 2048
+FLOPS = 2 * 2 * TOKENS * K * N
+BYTES = 2 * (TOKENS * K + N * K + 16 * 8 + TOKENS * N) + 4 * (TOKENS * K + N * K)
+
+F32 = mybir.dt.float32
+BF16 = mybir.dt.bfloat16
+U32 = mybir.dt.uint32
+U8 = mybir.dt.uint8
+E4M3 = mybir.dt.float8_e4m3fn_x4
+E5M2 = mybir.dt.float8_e5m2_x4
+COPY = mybir.ActivationFunctionType.Copy
+MULT = mybir.AluOpType.mult
+
+P = 128
+PACK = 4
+HALF = 512
+CHUNK = 512
+BANKS = 8
+OUT_RING = 12
+V_EVAC = (2, 6)
+
+
+def tile_fp8columnparallellinear_v_kernel(tc, x, weight, weight_scale_inv, bias, grad_out, out_0, out_1):
+    nc = tc.nc
+    x_v = x.rearrange("(g p j) k -> g p j k", p=P, j=PACK)
+    g_v = grad_out.rearrange("(g p j) n -> g p j n", p=P, j=PACK)
+    w_v = weight.rearrange("(g p j) k -> g p j k", p=P, j=PACK)
+    o0_v = out_0.rearrange("(g p j) k -> g j p k", p=P, j=PACK)
+
+    with ExitStack() as ctx:
+        raw = ctx.enter_context(tc.tile_pool(name="raw", bufs=1))
+        keep = ctx.enter_context(tc.tile_pool(name="keep", bufs=1))
+        stage = ctx.enter_context(tc.tile_pool(name="stage", bufs=1))
+        psum = ctx.enter_context(tc.psum_pool(name="psum", bufs=1))
+        ctx.enter_context(tc.manual_schedule())
+
+        counters = {}
+
+        def ring(pool, label, count, shape, dtype):
+            i = counters.get(label, 0)
+            counters[label] = i + 1
+            return pool.tile(shape, dtype, name=label + str(i % count), align_bytes=256)
+
+        def bank():
+            i = counters.get("bank", 0)
+            counters["bank"] = i + 1
+            return psum.tile([P, 512], F32, name="bank" + str(i % BANKS))
+
+        xq = keep.tile([P, 2, K], U32, align_bytes=256, name="xq")
+        xs = keep.tile([P, 2, K], U8, align_bytes=256, name="xs")
+        gq = keep.tile([P, 2, N], U32, align_bytes=256, name="gq")
+        gs = keep.tile([P, 2, N], U8, align_bytes=256, name="gs")
+        gtq = keep.tile([P, 4, TOKENS], U32, align_bytes=256, name="gtq")
+        gts = keep.tile([P, 4, TOKENS], U8, align_bytes=256, name="gts")
+        wq = keep.tile([P, 4, K], U32, align_bytes=256, name="wq")
+        ws = keep.tile([P, 4, K], U8, align_bytes=256, name="ws")
+        ident = keep.tile([P, P], F32, name="ident")
+        ones = keep.tile([P, P], BF16, name="ones")
+        srow = keep.tile([P, P], BF16, name="srow")
+        sc = keep.tile([P, P], F32, name="sc")
+        sw = keep.tile([P, 4, 8], F32, name="sw")
+        dummy = keep.tile([P, 1], F32, name="dummy")
+
+        x_raw = [raw.tile([P, PACK, K], BF16, name="raw" + str(i)) for i in range(2)]
+        g_raw = [[raw.tile([P, PACK, 1024], BF16, name="raw" + str(2 + 2 * c + i)) for i in range(2)] for c in range(2)]
+        w_raw = [raw.tile([P, PACK, K], BF16, name="raw" + str(6 + i)) for i in range(2)]
+
+        nc.vector.memset(srow[:], 0.0)
+        nc.vector.memset(ones[:], 1.0)
+        nc.vector.memset(dummy[:], 0.0)
+        nc.scalar.dma_start(out=srow[0:1, :], in_=weight_scale_inv.rearrange("(o a) b -> o (a b)", o=1))
+        nc.scalar.activation(out=dummy[:], in_=dummy[:], func=COPY)
+        make_identity(nc, ident[:])
+
+        def load_x(h, g):
+            nc.sync.dma_start(out=x_raw[g][:, :, h * HALF:(h + 1) * HALF], in_=x_v[g][:, :, h * HALF:(h + 1) * HALF])
+
+        def load_g(c0, width, g):
+            tile = g_raw[c0 // 1024][g]
+            a = c0 % 1024
+            nc.sync.dma_start(out=tile[:, :, a:a + width], in_=g_v[g][:, :, c0:c0 + width])
+
+        load_x(0, 0)
+        load_x(0, 1)
+        load_g(0, 512, 0)
+        load_g(0, 512, 1)
+        load_x(1, 0)
+        load_x(1, 1)
+        load_g(512, 512, 0)
+        load_g(512, 512, 1)
+        load_g(1024, 1024, 0)
+        load_g(1024, 1024, 1)
+        for i in range(2):
+            nc.sync.dma_start(out=w_raw[i][:], in_=w_v[i])
+
+        def lay(tile):
+            return tile.rearrange("p (c i t) -> p c t i", i=4, t=PACK)
+
+        def cols(src):
+            return src.rearrange("p t (c i) -> p c t i", i=4)
+
+        staged = {}
+
+        def copy_on(engine, out, src):
+            if engine == "v":
+                nc.vector.tensor_copy(out=out, in_=src)
+            else:
+                nc.scalar.copy(out=out, in_=src)
+
+        def ix(h, g, engine):
+            t = ring(stage, "in", 5, [P, 2048], BF16)
+            staged["x", h, g] = t
+            copy_on(engine, lay(t[:]), cols(x_raw[g][:, :, h * HALF:(h + 1) * HALF]))
+
+        def qx(h, g):
+            s = slice(h * HALF, (h + 1) * HALF)
+            nc.vector.quantize_mx(out=xq[:, g, s].bitcast(E4M3), scales=xs[:, g, s], in_=staged["x", h, g][:])
+
+        def ig(c, g, engine="v"):
+            t = ring(stage, "in", 5, [P, 2048], BF16)
+            staged["g", c, g] = t
+            a = c * CHUNK % 1024
+            copy_on(engine, lay(t[:]), cols(g_raw[c // 2][g][:, :, a:a + CHUNK]))
+
+        def qg(c, g):
+            s = slice(c * CHUNK, (c + 1) * CHUNK)
+            nc.vector.quantize_mx(out=gq[:, g, s].bitcast(E5M2), scales=gs[:, g, s], in_=staged["g", c, g][:])
+
+        def iw(g, h, engine):
+            t = ring(stage, "in", 5, [P, 2048], BF16)
+            staged["w", g, h] = t
+            for b in range(4):
+                kb = 4 * h + b
+                dst = lay(t[:, b * 512:(b + 1) * 512])
+                src = cols(w_raw[g][:, :, kb * P:(kb + 1) * P])
+                if engine == "v":
+                    nc.vector.tensor_scalar(out=dst, in0=src, scalar1=sw[:, g, kb:kb + 1], scalar2=None, op0=MULT)
+                else:
+                    nc.scalar.activation(out=dst, in_=src, func=COPY, scale=sw[:, g, kb:kb + 1])
+
+        def qw(g, h):
+            s = slice(h * HALF, (h + 1) * HALF)
+            nc.vector.quantize_mx(out=wq[:, g, s].bitcast(E4M3), scales=ws[:, g, s], in_=staged["w", g, h][:])
+
+        def transposes(c):
+            banks = []
+            for pair in range(4):
+                t = bank()
+                banks.append(t)
+                for b in range(2):
+                    tb = 2 * pair + b
+                    a = c * CHUNK % 1024
+                    words = g_raw[c // 2][tb // 4][:, tb % 4, a:a + CHUNK].bitcast(F32)
+                    for u in range(2):
+                        o = (2 * b + u) * P
+                        nc.tensor.transpose(t[:, o:o + P], words[:, u:256:2], ident[:])
+            staged["T", c] = banks
+
+        def cgt(c, pair, engine):
+            half = pair // 2
+            if pair % 2 == 0:
+                staged["gt", c, half] = ring(stage, "gt", 4, [P, 2048], BF16)
+            t = staged["gt", c, half]
+            o = (pair % 2) * 1024
+            dst = t[:, o:o + 1024].bitcast(F32).rearrange("p (b r u) -> p b r u", b=2, u=2)
+            src = staged["T", c][pair][:].rearrange("p (b u r) -> p b r u", b=2, u=2)
+            copy_on(engine, dst, src)
+
+        def qgt(c, half):
+            s = slice(half * 512, (half + 1) * 512)
+            nc.vector.quantize_mx(out=gtq[:, c, s].bitcast(E5M2), scales=gts[:, c, s], in_=staged["gt", c, half][:])
+
+        def mx1(acc, nb, h, g):
+            n_s = slice(nb * P, (nb + 1) * P)
+            k_s = slice(h * HALF, (h + 1) * HALF)
+            nc.tensor.matmul_mx(out=acc[:], lhsT=gq[:, g, n_s].bitcast(E5M2), lhsT_scale=gs[:, g, n_s],
+                                rhs=xq[:, g, k_s].bitcast(E4M3), rhs_scale=xs[:, g, k_s],
+                                start=(g == 0), stop=(g == 1))
+
+        out_tiles = {}
+
+        def e1(acc, nb, h, engine):
+            if nb not in out_tiles:
+                out_tiles[nb] = ring(stage, "out", OUT_RING, [P, 1024], F32)
+            o = out_tiles[nb]
+            if engine == "v":
+                a = nb * 8 + 4 * h
+                nc.vector.tensor_tensor(
+                    out=o[:, h * HALF:(h + 1) * HALF].rearrange("p (b k) -> p b k", b=4),
+                    in0=acc[:].rearrange("p (b k) -> p b k", b=4),
+                    in1=sc[:, a:a + 4].unsqueeze(2).to_broadcast([P, 4, P]), op=MULT)
+            else:
+                for b in range(4):
+                    kb = 4 * h + b
+                    nc.scalar.activation(out=o[:, kb * P:(kb + 1) * P], in_=acc[:, b * P:(b + 1) * P], func=COPY,
+                                         scale=sc[:, nb * 8 + kb:nb * 8 + kb + 1])
+
+        def store1(nb):
+            nc.sync.dma_start(out=out_1[nb * P:(nb + 1) * P, :], in_=out_tiles[nb][:])
+
+        def mx0(acc, tb, h, c):
+            t_s = slice(tb * P, (tb + 1) * P)
+            k_s = slice(h * HALF, (h + 1) * HALF)
+            nc.tensor.matmul_mx(out=acc[:], lhsT=gtq[:, c, t_s].bitcast(E5M2), lhsT_scale=gts[:, c, t_s],
+                                rhs=wq[:, c, k_s].bitcast(E4M3), rhs_scale=ws[:, c, k_s],
+                                start=(c == 0), stop=(c == 3))
+
+        def e0(acc, tb, h, engine):
+            o = ring(stage, "out", OUT_RING, [P, 512], F32)
+            copy_on(engine, o[:], acc[:])
+            nc.sync.dma_start(out=o0_v[tb // 4][tb % 4][:, h * HALF:(h + 1) * HALF], in_=o[:])
+
+        sb = bank()
+        nc.tensor.matmul(sb[:, 0:P], lhsT=ones[:], rhs=srow[:], start=True, stop=True)
+        nc.scalar.copy(out=sc[:], in_=sb[:, 0:P])
+        for q in range(4):
+            r = slice(32 * q, 32 * q + 32)
+            nc.gpsimd.tensor_copy(out=sw[r, :, :], in_=sc[r, :].rearrange("p (g q k) -> p g q k", g=4, q=4)[:, :, q, :])
+
+        ix(0, 0, "v")
+        ix(0, 1, "s")
+        transposes(0)
+        ig(0, 0)
+        qx(0, 0)
+        ig(0, 1)
+        qg(0, 0)
+        qx(0, 1)
+        qg(0, 1)
+        for pair in range(4):
+            cgt(0, pair, "s")
+
+        accs = [bank() for nb in range(4)]
+        for g in range(2):
+            for nb in range(4):
+                mx1(accs[nb], nb, 0, g)
+        ix(1, 0, "v")
+        ix(1, 1, "s")
+        e1(accs[0], 0, 0, "v")
+        qx(1, 0)
+        e1(accs[1], 1, 0, "s")
+        e1(accs[2], 2, 0, "s")
+        qx(1, 1)
+        e1(accs[3], 3, 0, "s")
+        w_raw = w_raw + [raw.tile([P, PACK, K], BF16, name="raw" + str(i)) for i in range(2)]
+        for i in range(2, 4):
+            nc.sync.dma_start(out=w_raw[i][:], in_=w_v[i])
+        transposes(1)
+        ig(1, 0)
+        qgt(0, 0)
+        ig(1, 1)
+        qgt(0, 1)
+        for pair in range(4):
+            cgt(1, pair, "s")
+        accs = [bank() for nb in range(4)]
+        for nb in range(4):
+            for g in range(2):
+                mx1(accs[nb], nb, 1, g)
+        qg(1, 0)
+        e1(accs[0], 0, 1, "s")
+        store1(0)
+        e1(accs[1], 1, 1, "v")
+        store1(1)
+        qg(1, 1)
+        e1(accs[2], 2, 1, "s")
+        store1(2)
+        qgt(1, 0)
+        e1(accs[3], 3, 1, "s")
+        store1(3)
+        qgt(1, 1)
+
+        for c in range(1, 4):
+            if c < 3:
+                transposes(c + 1)
+                for pair in range(4):
+                    cgt(c + 1, pair, "s")
+                vtasks = [(ig, c + 1, 0), (ig, c + 1, 1), None, (qg, c + 1, 0), (qgt, c + 1, 0), (qg, c + 1, 1), None, (qgt, c + 1, 1)]
+            else:
+                vtasks = [(iw, 0, 0, "v"), (iw, 1, 0, "v"), None, (qw, 0, 0), None, (iw, 2, 0, "v"), None, (qw, 1, 0)]
+            for i in range(8):
+                nb = 4 * c + i // 2
+                h = i % 2
+                acc = bank()
+                for g in range(2):
+                    mx1(acc, nb, h, g)
+                if vtasks[i]:
+                    vtasks[i][0](*vtasks[i][1:])
+                e1(acc, nb, h, "v" if i in V_EVAC else "s")
+                if h == 1:
+                    store1(nb)
+
+        vtasks = [[(iw, 0, 1, "v"), (qw, 2, 0)], [(iw, 1, 1, "v"), (qw, 3, 0)], [(iw, 2, 1, "v"), (qw, 0, 1)],
+                  [(qw, 1, 1)]]
+        accs = [bank() for tb in range(8)]
+        iw(3, 0, "s")
+        for c in range(4):
+            for tb in range(8):
+                mx0(accs[tb], tb, 0, c)
+            for task in vtasks[c]:
+                task[0](*task[1:])
+        for tb in range(8):
+            e0(accs[tb], tb, 0, "v" if tb % 2 else "s")
+            if tb == 1:
+                iw(3, 1, "v")
+            if tb == 3:
+                qw(2, 1)
+            if tb == 5:
+                qw(3, 1)
+        accs = [bank() for tb in range(4)]
+        for c in range(4):
+            for tb in range(4):
+                mx0(accs[tb], tb, 1, c)
+        for tb in range(4):
+            e0(accs[tb], tb, 1, "v" if tb % 2 else "s")
+        for tb in range(4, 8):
+            acc = bank()
+            for c in range(4):
+                mx0(acc, tb, 1, c)
+            e0(acc, tb, 1, "v" if tb % 2 else "s")

@@ -21,7 +21,7 @@ PACK = 4
 HALF = 512
 CHUNK = 512
 BANKS = 8
-OUT_RING = 12
+OUT_RING = 11
 V_EVAC = (2, 6)
 
 
@@ -66,36 +66,39 @@ def tile_fp8columnparallellinear_v_kernel(tc, x, weight, weight_scale_inv, bias,
         sw = keep.tile([P, 4, 8], F32, name="sw")
         dummy = keep.tile([P, 1], F32, name="dummy")
 
-        x_raw = [raw.tile([P, PACK, K], BF16, name="raw" + str(i)) for i in range(2)]
-        g_raw = [[raw.tile([P, PACK, 1024], BF16, name="raw" + str(2 + 2 * c + i)) for i in range(2)] for c in range(2)]
-        w_raw = [raw.tile([P, PACK, K], BF16, name="raw" + str(6 + i)) for i in range(2)]
+        x_raw = {(h, g): raw.tile([P, PACK, HALF], BF16, name="x_raw%d%d" % (h, g)) for h in range(2) for g in range(2)}
+        g_raw = {(c, g): raw.tile([P, PACK, CHUNK], BF16, name="g_raw%d%d" % (c, g)) for c in range(2) for g in range(2)}
+        g_wide = [raw.tile([P, PACK, 2 * CHUNK], BF16, name="g_wide%d" % g) for g in range(2)]
+        w_raw = [raw.tile([P, PACK, K], BF16, name="w_raw%d" % i) for i in range(4)]
+        for g in range(2):
+            g_raw[2, g] = g_wide[g][:, :, 0:CHUNK]
+            g_raw[3, g] = g_wide[g][:, :, CHUNK:2 * CHUNK]
 
         nc.vector.memset(srow[:], 0.0)
         nc.vector.memset(ones[:], 1.0)
         nc.vector.memset(dummy[:], 0.0)
-        nc.scalar.dma_start(out=srow[0:1, :], in_=weight_scale_inv.rearrange("(o a) b -> o (a b)", o=1))
         nc.scalar.activation(out=dummy[:], in_=dummy[:], func=COPY)
         make_identity(nc, ident[:])
 
         def load_x(h, g):
-            nc.sync.dma_start(out=x_raw[g][:, :, h * HALF:(h + 1) * HALF], in_=x_v[g][:, :, h * HALF:(h + 1) * HALF])
+            nc.sync.dma_start(out=x_raw[h, g][:], in_=x_v[g][:, :, h * HALF:(h + 1) * HALF])
 
         def load_g(c0, width, g):
-            tile = g_raw[c0 // 1024][g]
-            a = c0 % 1024
-            nc.sync.dma_start(out=tile[:, :, a:a + width], in_=g_v[g][:, :, c0:c0 + width])
+            tile = g_raw[c0 // CHUNK, g] if width == CHUNK else g_wide[g]
+            nc.sync.dma_start(out=tile[:], in_=g_v[g][:, :, c0:c0 + width])
 
         load_x(0, 0)
         load_x(0, 1)
         load_g(0, 512, 0)
         load_g(0, 512, 1)
+        nc.sync.dma_start(out=srow[0:1, :], in_=weight_scale_inv.rearrange("(o a) b -> o (a b)", o=1))
         load_x(1, 0)
         load_x(1, 1)
         load_g(512, 512, 0)
         load_g(512, 512, 1)
         load_g(1024, 1024, 0)
         load_g(1024, 1024, 1)
-        for i in range(2):
+        for i in range(4):
             nc.sync.dma_start(out=w_raw[i][:], in_=w_v[i])
 
         def lay(tile):
@@ -115,7 +118,7 @@ def tile_fp8columnparallellinear_v_kernel(tc, x, weight, weight_scale_inv, bias,
         def ix(h, g, engine):
             t = ring(stage, "in", 5, [P, 2048], BF16)
             staged["x", h, g] = t
-            copy_on(engine, lay(t[:]), cols(x_raw[g][:, :, h * HALF:(h + 1) * HALF]))
+            copy_on(engine, lay(t[:]), cols(x_raw[h, g][:]))
 
         def qx(h, g):
             s = slice(h * HALF, (h + 1) * HALF)
@@ -124,8 +127,7 @@ def tile_fp8columnparallellinear_v_kernel(tc, x, weight, weight_scale_inv, bias,
         def ig(c, g, engine="v"):
             t = ring(stage, "in", 5, [P, 2048], BF16)
             staged["g", c, g] = t
-            a = c * CHUNK % 1024
-            copy_on(engine, lay(t[:]), cols(g_raw[c // 2][g][:, :, a:a + CHUNK]))
+            copy_on(engine, lay(t[:]), cols(g_raw[c, g][:, :, :]))
 
         def qg(c, g):
             s = slice(c * CHUNK, (c + 1) * CHUNK)
@@ -154,8 +156,7 @@ def tile_fp8columnparallellinear_v_kernel(tc, x, weight, weight_scale_inv, bias,
                 banks.append(t)
                 for b in range(2):
                     tb = 2 * pair + b
-                    a = c * CHUNK % 1024
-                    words = g_raw[c // 2][tb // 4][:, tb % 4, a:a + CHUNK].bitcast(F32)
+                    words = g_raw[c, tb // 4][:, tb % 4, :].bitcast(F32)
                     for u in range(2):
                         o = (2 * b + u) * P
                         nc.tensor.transpose(t[:, o:o + P], words[:, u:256:2], ident[:])
@@ -215,12 +216,6 @@ def tile_fp8columnparallellinear_v_kernel(tc, x, weight, weight_scale_inv, bias,
             copy_on(engine, o[:], acc[:])
             nc.sync.dma_start(out=o0_v[tb // 4][tb % 4][:, h * HALF:(h + 1) * HALF], in_=o[:])
 
-        sb = bank()
-        nc.tensor.matmul(sb[:, 0:P], lhsT=ones[:], rhs=srow[:], start=True, stop=True)
-        nc.scalar.copy(out=sc[:], in_=sb[:, 0:P])
-        for q in range(4):
-            r = slice(32 * q, 32 * q + 32)
-            nc.gpsimd.tensor_copy(out=sw[r, :, :], in_=sc[r, :].rearrange("p (g q k) -> p g q k", g=4, q=4)[:, :, q, :])
 
         ix(0, 0, "v")
         ix(0, 1, "s")
@@ -231,6 +226,12 @@ def tile_fp8columnparallellinear_v_kernel(tc, x, weight, weight_scale_inv, bias,
         qg(0, 0)
         qx(0, 1)
         qg(0, 1)
+        sb = bank()
+        nc.tensor.matmul(sb[:, 0:P], lhsT=ones[:], rhs=srow[:], start=True, stop=True)
+        nc.scalar.copy(out=sc[:], in_=sb[:, 0:P])
+        for q in range(4):
+            r = slice(32 * q, 32 * q + 32)
+            nc.gpsimd.tensor_copy(out=sw[r, :, :], in_=sc[r, :].rearrange("p (g q k) -> p g q k", g=4, q=4)[:, :, q, :])
         for pair in range(4):
             cgt(0, pair, "s")
 
@@ -246,9 +247,6 @@ def tile_fp8columnparallellinear_v_kernel(tc, x, weight, weight_scale_inv, bias,
         e1(accs[2], 2, 0, "s")
         qx(1, 1)
         e1(accs[3], 3, 0, "s")
-        w_raw = w_raw + [raw.tile([P, PACK, K], BF16, name="raw" + str(i)) for i in range(2)]
-        for i in range(2, 4):
-            nc.sync.dma_start(out=w_raw[i][:], in_=w_v[i])
         transposes(1)
         ig(1, 0)
         qgt(0, 0)

@@ -21,8 +21,57 @@ PACK = 4
 HALF = 512
 CHUNK = 512
 BANKS = 8
-OUT_RING = 11
-V_EVAC = (2, 6)
+IN_BUFS, GT_BUFS, OUT_BUFS = 6, 8, 10
+LOADS = ("g 0 1 0", "x 0 1 0", "s 0", "x 0 1 1", "g 0 1 1", "x 1 1 0", "x 1 1 1", "g 1 1 0", "g 1 1 1", "g 2 2 0", "g 2 2 1", "w 0", "w 1",)
+
+PE_SEQ = (
+    "D 4, T 0 0, D 6, M1 0 0 0, M1 1 0 0, M1 2 0 0, M1 3 0 0, S",
+    "T 0 1, M1 0 0 1, M1 1 0 1, M1 2 0 1, M1 3 0 1, T 1 0, M1 0 1 0, M1 0 1 1",
+    "M1 1 1 0, M1 1 1 1, T 1 1, M1 2 1 0, M1 2 1 1, M1 3 1 0, M1 3 1 1, T 2 0",
+    "M1 4 0 0, M1 4 0 1, M1 4 1 0, M1 4 1 1, M1 5 0 0, M1 5 0 1, M1 5 1 0, M1 5 1 1",
+    "T 2 1, M1 6 0 0, M1 6 0 1, M1 6 1 0, M1 6 1 1, M1 7 0 0, M1 7 0 1, M1 7 1 0",
+    "M1 7 1 1, T 3 0, M1 8 0 0, M1 8 0 1, M1 8 1 0, M1 8 1 1, M1 9 0 0, M1 9 0 1",
+    "M1 9 1 0, M1 9 1 1, T 3 1, M1 10 0 0, M1 10 0 1, M1 10 1 0, M1 10 1 1, M1 11 0 0",
+    "M1 11 0 1, M1 11 1 0, M1 11 1 1, M1 12 0 0, M1 12 0 1, M1 12 1 0, M1 12 1 1, M1 13 0 0",
+    "M1 13 0 1, M1 13 1 0, M1 13 1 1, M1 14 0 0, M1 14 0 1, M1 14 1 0, M1 14 1 1, M1 15 0 0",
+    "M1 15 0 1, M1 15 1 0, M1 15 1 1, M0 0 0 0, M0 0 1 0, M0 0 2 0, M0 0 3 0, M0 0 4 0",
+    "M0 0 5 0, M0 0 6 0, M0 0 7 0, M0 1 0 0, M0 1 1 0, M0 1 2 0, M0 1 3 0, M0 1 4 0",
+    "M0 1 5 0, M0 1 6 0, M0 1 7 0, M0 2 0 0, M0 2 1 0, M0 2 2 0, M0 2 3 0, M0 2 4 0",
+    "M0 2 5 0, M0 2 6 0, M0 2 7 0, M0 3 0 0, M0 3 1 0, M0 3 2 0, M0 3 3 0, M0 3 4 0",
+    "M0 3 5 0, M0 3 6 0, M0 3 7 0, M0 0 0 1, M0 0 1 1, M0 0 2 1, M0 0 3 1, M0 1 0 1",
+    "M0 1 1 1, M0 1 2 1, M0 1 3 1, M0 2 0 1, M0 2 1 1, M0 2 2 1, M0 2 3 1, M0 3 0 1",
+    "M0 3 1 1, M0 3 2 1, M0 3 3 1, M0 0 4 1, M0 1 4 1, M0 2 4 1, M0 3 4 1, M0 0 5 1",
+    "M0 1 5 1, M0 2 5 1, M0 3 5 1, M0 0 6 1, M0 1 6 1, M0 2 6 1, M0 3 6 1, M0 0 7 1",
+    "M0 1 7 1, M0 2 7 1, M0 3 7 1",
+)
+V_SEQ = (
+    "Ig 0 0, Ix 0 0, Qg 0 0, Qx 0 0, Ig 0 1, sc, Qx 0 1, Qg 0 1",
+    "Ix 1 1, Qx 1 0, Qx 1 1, Ig 1 0, Ig 1 1, E1 0 1, Qg 1 1, Qt 0 0",
+    "Qg 1 0, Qt 1 0, Ig 3 0, Ig 2 1, Ig 2 0, E1 6 0, Qg 3 0, Qg 2 0",
+    "Qg 2 1, E1 7 1, Iw 1 0, Iw 0 0, Ig 3 1, Qw 0 0, Qg 3 1, Qt 2 0",
+    "C 3 1 1, E1 11 1, E1 1 1, E1 12 0, Iw 2 0, E1 14 0, Qt 0 1, E1 13 1",
+    "E1 14 1, Qw 1 0, Qw 2 0, Qt 1 1, Qt 3 1, Qt 2 1, Qt 3 0, Iw 1 1",
+    "Qw 3 0, Qw 1 1, Qw 0 1, E0 0 0, E0 1 0, E0 4 0, Qw 2 1, Iw 3 1",
+    "Qw 3 1",
+)
+S_SEQ = (
+    "C 0 0 1, C 0 0 0, Ix 0 1, Ix 1 0, E1 1 0, C 0 1 1, E1 0 0, C 1 0 1",
+    "E1 2 0, C 1 1 0, E1 3 0, C 1 0 0, C 0 1 0, C 2 0 0, C 1 1 1, E1 3 1",
+    "E1 4 1, C 2 0 1, E1 4 0, E1 5 0, C 2 1 0, E1 2 1, E1 7 0, C 2 1 1",
+    "E1 5 1, E1 8 0, C 3 0 0, E1 6 1, E1 8 1, C 3 0 1, E1 9 0, E1 9 1",
+    "E1 10 0, C 3 1 0, E1 11 0, E1 12 1, E1 10 1, E1 13 0, E1 15 0, E1 15 1",
+    "Iw 3 0, Iw 0 1, Iw 2 1, E0 7 0, E0 6 0, E0 3 0, E0 5 0, E0 0 1",
+    "E0 3 1, E0 1 1, E0 2 0, E0 2 1, E0 5 1, E0 4 1, E0 6 1, E0 7 1",
+)
+
+
+def parse(text):
+    words = text.split(" ")
+    return tuple([words[0]] + [int(w) for w in words[1:]])
+
+
+def items(lines):
+    return [parse(t) for line in lines for t in line.split(", ")]
 
 
 def tile_fp8columnparallellinear_v_kernel(tc, x, weight, weight_scale_inv, bias, grad_out, out_0, out_1):
@@ -33,81 +82,82 @@ def tile_fp8columnparallellinear_v_kernel(tc, x, weight, weight_scale_inv, bias,
     o0_v = out_0.rearrange("(g p j) k -> g j p k", p=P, j=PACK)
 
     with ExitStack() as ctx:
-        raw = ctx.enter_context(tc.tile_pool(name="raw", bufs=1))
-        keep = ctx.enter_context(tc.tile_pool(name="keep", bufs=1))
-        stage = ctx.enter_context(tc.tile_pool(name="stage", bufs=1))
+        sbuf = ctx.enter_context(tc.tile_pool(name="sbuf", bufs=1))
         psum = ctx.enter_context(tc.psum_pool(name="psum", bufs=1))
         ctx.enter_context(tc.manual_schedule())
 
-        counters = {}
+        def tile(name, shape, dtype):
+            return sbuf.tile(shape, dtype, name=name, align_bytes=64)
 
-        def ring(pool, label, count, shape, dtype):
-            i = counters.get(label, 0)
-            counters[label] = i + 1
-            return pool.tile(shape, dtype, name=label + str(i % count), align_bytes=256)
+        xq, xs = tile("xq", [P, 2, K], U32), tile("xs", [P, 2, K], U8)
+        gq, gs = tile("gq", [P, 2, N], U32), tile("gs", [P, 2, N], U8)
+        gtq, gts = tile("gtq", [P, 4, TOKENS], U32), tile("gts", [P, 4, TOKENS], U8)
+        wq, ws = tile("wq", [P, 4, K], U32), tile("ws", [P, 4, K], U8)
+        ident = tile("ident", [P, P], F32)
+        ones = tile("ones", [P, P], BF16)
+        warm = tile("warm", [P, 512], BF16)
+        srow = tile("srow", [P, P], BF16)
+        sc = tile("sc", [P, P], F32)
+        sw = tile("sw", [P, 4, 8], F32)
+        dummy = tile("dummy", [P, 1], F32)
 
-        def bank():
-            i = counters.get("bank", 0)
-            counters["bank"] = i + 1
-            return psum.tile([P, 512], F32, name="bank" + str(i % BANKS))
+        x_pair = [tile("x_or_w%d" % h, [P, 2, PACK, HALF], BF16) for h in range(2)]
+        g_tiles = {}
+        w_raw = {g: tile("w_raw%d" % g, [P, PACK, K], BF16) for g in range(2)}
 
-        xq = keep.tile([P, 2, K], U32, align_bytes=256, name="xq")
-        xs = keep.tile([P, 2, K], U8, align_bytes=256, name="xs")
-        gq = keep.tile([P, 2, N], U32, align_bytes=256, name="gq")
-        gs = keep.tile([P, 2, N], U8, align_bytes=256, name="gs")
-        gtq = keep.tile([P, 4, TOKENS], U32, align_bytes=256, name="gtq")
-        gts = keep.tile([P, 4, TOKENS], U8, align_bytes=256, name="gts")
-        wq = keep.tile([P, 4, K], U32, align_bytes=256, name="wq")
-        ws = keep.tile([P, 4, K], U8, align_bytes=256, name="ws")
-        ident = keep.tile([P, P], F32, name="ident")
-        ones = keep.tile([P, P], BF16, name="ones")
-        srow = keep.tile([P, P], BF16, name="srow")
-        sc = keep.tile([P, P], F32, name="sc")
-        sw = keep.tile([P, 4, 8], F32, name="sw")
-        dummy = keep.tile([P, 1], F32, name="dummy")
+        def x_raw(h, g):
+            return x_pair[h][:, g, :, :]
 
-        x_raw = {(h, g): raw.tile([P, PACK, HALF], BF16, name="x_raw%d%d" % (h, g)) for h in range(2) for g in range(2)}
-        g_raw = {(c, g): raw.tile([P, PACK, CHUNK], BF16, name="g_raw%d%d" % (c, g)) for c in range(2) for g in range(2)}
-        g_wide = [raw.tile([P, PACK, 2 * CHUNK], BF16, name="g_wide%d" % g) for g in range(2)]
-        w_raw = [raw.tile([P, PACK, K], BF16, name="w_raw%d" % i) for i in range(4)]
-        for g in range(2):
-            g_raw[2, g] = g_wide[g][:, :, 0:CHUNK]
-            g_raw[3, g] = g_wide[g][:, :, CHUNK:2 * CHUNK]
+        def g_raw(c, g):
+            t, first = g_tiles[c, g]
+            return t[:, :, (c - first) * CHUNK:(c - first + 1) * CHUNK]
 
-        nc.vector.memset(srow[:], 0.0)
         nc.vector.memset(ones[:], 1.0)
+        nc.vector.memset(warm[:], 0.0)
+        nc.vector.memset(srow[:], 0.0)
         nc.vector.memset(dummy[:], 0.0)
         nc.scalar.activation(out=dummy[:], in_=dummy[:], func=COPY)
         make_identity(nc, ident[:])
 
-        def load_x(h, g):
-            nc.sync.dma_start(out=x_raw[h, g][:], in_=x_v[g][:, :, h * HALF:(h + 1) * HALF])
+        for load in items(LOADS):
+            kind, a = load[0], load[1]
+            if kind == "x":
+                nc.sync.dma_start(out=x_raw(a, load[3]), in_=x_v[load[3]][:, :, a * HALF:(a + 1) * HALF])
+            elif kind == "g":
+                t = tile("g_raw%d%d" % (a, load[3]), [P, PACK, load[2] * CHUNK], BF16)
+                for c in range(a, a + load[2]):
+                    g_tiles[c, load[3]] = (t, a)
+                nc.sync.dma_start(out=t[:], in_=g_v[load[3]][:, :, a * CHUNK:(a + load[2]) * CHUNK])
+            elif kind == "s":
+                nc.sync.dma_start(out=srow[0:1, :], in_=weight_scale_inv.rearrange("(o a) b -> o (a b)", o=1))
+            else:
+                nc.sync.dma_start(out=w_raw[a][:], in_=w_v[a])
 
-        def load_g(c0, width, g):
-            tile = g_raw[c0 // CHUNK, g] if width == CHUNK else g_wide[g]
-            nc.sync.dma_start(out=tile[:], in_=g_v[g][:, :, c0:c0 + width])
+        free = {"in": list(range(IN_BUFS)), "gt": list(range(GT_BUFS)), "out": list(range(OUT_BUFS)), "bank": list(range(BANKS))}
+        slot_of = {}
+        held = {}
+        done = set()
 
-        load_x(0, 0)
-        load_x(0, 1)
-        load_g(0, 512, 0)
-        load_g(0, 512, 1)
-        nc.sync.dma_start(out=srow[0:1, :], in_=weight_scale_inv.rearrange("(o a) b -> o (a b)", o=1))
-        load_x(1, 0)
-        load_x(1, 1)
-        load_g(512, 512, 0)
-        load_g(512, 512, 1)
-        load_g(1024, 1024, 0)
-        load_g(1024, 1024, 1)
-        for i in range(4):
-            nc.sync.dma_start(out=w_raw[i][:], in_=w_v[i])
+        def take(kind, key, shape, dtype):
+            slot = free[kind][0]
+            free[kind].remove(slot)
+            slot_of[key] = (kind, slot)
+            name = kind + str(slot)
+            if kind == "bank":
+                held[key] = psum.tile(shape, dtype, name=name)
+            else:
+                held[key] = tile(name, shape, dtype)
+            return held[key]
 
-        def lay(tile):
-            return tile.rearrange("p (c i t) -> p c t i", i=4, t=PACK)
+        def give(key):
+            kind, slot = slot_of[key]
+            free[kind].append(slot)
+
+        def lay(t):
+            return t.rearrange("p (c i t) -> p c t i", i=4, t=PACK)
 
         def cols(src):
             return src.rearrange("p t (c i) -> p c t i", i=4)
-
-        staged = {}
 
         def copy_on(engine, out, src):
             if engine == "v":
@@ -115,207 +165,172 @@ def tile_fp8columnparallellinear_v_kernel(tc, x, weight, weight_scale_inv, bias,
             else:
                 nc.scalar.copy(out=out, in_=src)
 
-        def ix(h, g, engine):
-            t = ring(stage, "in", 5, [P, 2048], BF16)
-            staged["x", h, g] = t
-            copy_on(engine, lay(t[:]), cols(x_raw[h, g][:]))
+        def needs(item):
+            kind = item[0]
+            a = item[1:]
+            if kind == "Iw":
+                return [("sc",)] + ([("Ix", a[0] - 2, 0), ("Ix", a[0] - 2, 1)] if a[0] > 1 else [])
+            if kind in ("Qx", "Qg", "Qw"):
+                return [("I" + kind[1],) + a]
+            if kind == "sc":
+                return [("S",)]
+            if kind == "C":
+                return [("T",) + a[:2]]
+            if kind == "Qt":
+                return [("C",) + a + (0,), ("C",) + a + (1,)]
+            if kind == "E1":
+                return [("M1",) + a + (1,), ("sc",)]
+            if kind == "E0":
+                return [("M0", 3) + a]
+            if kind == "M1":
+                return [("Qg", a[0] // 4, a[2]), ("Qx", a[1], a[2])]
+            if kind == "M0":
+                return [("Qw", a[0], a[2]), ("Qt", a[0], a[1] // 4)]
+            return []
 
-        def qx(h, g):
-            s = slice(h * HALF, (h + 1) * HALF)
-            nc.vector.quantize_mx(out=xq[:, g, s].bitcast(E4M3), scales=xs[:, g, s], in_=staged["x", h, g][:])
+        def has_slots(item):
+            kind = item[0]
+            if kind in ("Ix", "Ig", "Iw"):
+                return len(free["in"]) > 0
+            if kind == "C":
+                return ("gt",) + item[1:3] in held or len(free["gt"]) > 0
+            if kind == "E1":
+                return ("o",) + item[1:2] in held or len(free["out"]) > 0
+            if kind == "E0":
+                return len(free["out"]) > 0
+            if kind == "T":
+                return len(free["bank"]) > 1
+            if kind == "S" or (kind == "M1" and item[3] == 0) or (kind == "M0" and item[1] == 0):
+                return len(free["bank"]) > 0
+            return True
 
-        def ig(c, g, engine="v"):
-            t = ring(stage, "in", 5, [P, 2048], BF16)
-            staged["g", c, g] = t
-            copy_on(engine, lay(t[:]), cols(g_raw[c, g][:, :, :]))
-
-        def qg(c, g):
-            s = slice(c * CHUNK, (c + 1) * CHUNK)
-            nc.vector.quantize_mx(out=gq[:, g, s].bitcast(E5M2), scales=gs[:, g, s], in_=staged["g", c, g][:])
-
-        def iw(g, h, engine):
-            t = ring(stage, "in", 5, [P, 2048], BF16)
-            staged["w", g, h] = t
-            for b in range(4):
-                kb = 4 * h + b
-                dst = lay(t[:, b * 512:(b + 1) * 512])
-                src = cols(w_raw[g][:, :, kb * P:(kb + 1) * P])
-                if engine == "v":
-                    nc.vector.tensor_scalar(out=dst, in0=src, scalar1=sw[:, g, kb:kb + 1], scalar2=None, op0=MULT)
-                else:
-                    nc.scalar.activation(out=dst, in_=src, func=COPY, scale=sw[:, g, kb:kb + 1])
-
-        def qw(g, h):
-            s = slice(h * HALF, (h + 1) * HALF)
-            nc.vector.quantize_mx(out=wq[:, g, s].bitcast(E4M3), scales=ws[:, g, s], in_=staged["w", g, h][:])
-
-        def transposes(c):
-            banks = []
-            for pair in range(4):
-                t = bank()
-                banks.append(t)
-                for b in range(2):
-                    tb = 2 * pair + b
-                    words = g_raw[c, tb // 4][:, tb % 4, :].bitcast(F32)
-                    for u in range(2):
-                        o = (2 * b + u) * P
-                        nc.tensor.transpose(t[:, o:o + P], words[:, u:256:2], ident[:])
-            staged["T", c] = banks
-
-        def cgt(c, pair, engine):
-            half = pair // 2
-            if pair % 2 == 0:
-                staged["gt", c, half] = ring(stage, "gt", 4, [P, 2048], BF16)
-            t = staged["gt", c, half]
-            o = (pair % 2) * 1024
-            dst = t[:, o:o + 1024].bitcast(F32).rearrange("p (b r u) -> p b r u", b=2, u=2)
-            src = staged["T", c][pair][:].rearrange("p (b u r) -> p b r u", b=2, u=2)
-            copy_on(engine, dst, src)
-
-        def qgt(c, half):
-            s = slice(half * 512, (half + 1) * 512)
-            nc.vector.quantize_mx(out=gtq[:, c, s].bitcast(E5M2), scales=gts[:, c, s], in_=staged["gt", c, half][:])
-
-        def mx1(acc, nb, h, g):
-            n_s = slice(nb * P, (nb + 1) * P)
-            k_s = slice(h * HALF, (h + 1) * HALF)
-            nc.tensor.matmul_mx(out=acc[:], lhsT=gq[:, g, n_s].bitcast(E5M2), lhsT_scale=gs[:, g, n_s],
-                                rhs=xq[:, g, k_s].bitcast(E4M3), rhs_scale=xs[:, g, k_s],
-                                start=(g == 0), stop=(g == 1))
-
-        out_tiles = {}
-
-        def e1(acc, nb, h, engine):
-            if nb not in out_tiles:
-                out_tiles[nb] = ring(stage, "out", OUT_RING, [P, 1024], F32)
-            o = out_tiles[nb]
-            if engine == "v":
-                a = nb * 8 + 4 * h
-                nc.vector.tensor_tensor(
-                    out=o[:, h * HALF:(h + 1) * HALF].rearrange("p (b k) -> p b k", b=4),
-                    in0=acc[:].rearrange("p (b k) -> p b k", b=4),
-                    in1=sc[:, a:a + 4].unsqueeze(2).to_broadcast([P, 4, P]), op=MULT)
-            else:
+        def step(item, engine):
+            kind = item[0]
+            a = item[1:]
+            if kind in ("Ix", "Ig"):
+                t = take("in", item, [P, 2048], BF16)
+                copy_on(engine, lay(t[:]), cols(x_raw(*a) if kind == "Ix" else g_raw(*a)))
+                if kind == "Ix" and ("Ix", a[0], 1 - a[1]) in done:
+                    w_raw[2 + a[0]] = tile("x_or_w%d" % a[0], [P, PACK, K], BF16)
+                    nc.sync.dma_start(out=w_raw[2 + a[0]][:], in_=w_v[2 + a[0]])
+            elif kind == "Iw":
+                t = take("in", item, [P, 2048], BF16)
+                g, h = a
                 for b in range(4):
                     kb = 4 * h + b
-                    nc.scalar.activation(out=o[:, kb * P:(kb + 1) * P], in_=acc[:, b * P:(b + 1) * P], func=COPY,
-                                         scale=sc[:, nb * 8 + kb:nb * 8 + kb + 1])
-
-        def store1(nb):
-            nc.sync.dma_start(out=out_1[nb * P:(nb + 1) * P, :], in_=out_tiles[nb][:])
-
-        def mx0(acc, tb, h, c):
-            t_s = slice(tb * P, (tb + 1) * P)
-            k_s = slice(h * HALF, (h + 1) * HALF)
-            nc.tensor.matmul_mx(out=acc[:], lhsT=gtq[:, c, t_s].bitcast(E5M2), lhsT_scale=gts[:, c, t_s],
-                                rhs=wq[:, c, k_s].bitcast(E4M3), rhs_scale=ws[:, c, k_s],
-                                start=(c == 0), stop=(c == 3))
-
-        def e0(acc, tb, h, engine):
-            o = ring(stage, "out", OUT_RING, [P, 512], F32)
-            copy_on(engine, o[:], acc[:])
-            nc.sync.dma_start(out=o0_v[tb // 4][tb % 4][:, h * HALF:(h + 1) * HALF], in_=o[:])
-
-
-        ix(0, 0, "v")
-        ix(0, 1, "s")
-        transposes(0)
-        ig(0, 0)
-        qx(0, 0)
-        ig(0, 1)
-        qg(0, 0)
-        qx(0, 1)
-        qg(0, 1)
-        sb = bank()
-        nc.tensor.matmul(sb[:, 0:P], lhsT=ones[:], rhs=srow[:], start=True, stop=True)
-        nc.scalar.copy(out=sc[:], in_=sb[:, 0:P])
-        for q in range(4):
-            r = slice(32 * q, 32 * q + 32)
-            nc.gpsimd.tensor_copy(out=sw[r, :, :], in_=sc[r, :].rearrange("p (g q k) -> p g q k", g=4, q=4)[:, :, q, :])
-        for pair in range(4):
-            cgt(0, pair, "s")
-
-        accs = [bank() for nb in range(4)]
-        for g in range(2):
-            for nb in range(4):
-                mx1(accs[nb], nb, 0, g)
-        ix(1, 0, "v")
-        ix(1, 1, "s")
-        e1(accs[0], 0, 0, "v")
-        qx(1, 0)
-        e1(accs[1], 1, 0, "s")
-        e1(accs[2], 2, 0, "s")
-        qx(1, 1)
-        e1(accs[3], 3, 0, "s")
-        transposes(1)
-        ig(1, 0)
-        qgt(0, 0)
-        ig(1, 1)
-        qgt(0, 1)
-        for pair in range(4):
-            cgt(1, pair, "s")
-        accs = [bank() for nb in range(4)]
-        for nb in range(4):
-            for g in range(2):
-                mx1(accs[nb], nb, 1, g)
-        qg(1, 0)
-        e1(accs[0], 0, 1, "s")
-        store1(0)
-        e1(accs[1], 1, 1, "v")
-        store1(1)
-        qg(1, 1)
-        e1(accs[2], 2, 1, "s")
-        store1(2)
-        qgt(1, 0)
-        e1(accs[3], 3, 1, "s")
-        store1(3)
-        qgt(1, 1)
-
-        for c in range(1, 4):
-            if c < 3:
-                transposes(c + 1)
-                for pair in range(4):
-                    cgt(c + 1, pair, "s")
-                vtasks = [(ig, c + 1, 0), (ig, c + 1, 1), None, (qg, c + 1, 0), (qgt, c + 1, 0), (qg, c + 1, 1), None, (qgt, c + 1, 1)]
+                    dst = lay(t[:, b * 512:(b + 1) * 512])
+                    src = cols(w_raw[g][:, :, kb * P:(kb + 1) * P])
+                    if engine == "v":
+                        nc.vector.tensor_scalar(out=dst, in0=src, scalar1=sw[:, g, kb:kb + 1], scalar2=None, op0=MULT)
+                    else:
+                        nc.scalar.activation(out=dst, in_=src, func=COPY, scale=sw[:, g, kb:kb + 1])
+            elif kind == "Qx":
+                s = slice(a[0] * HALF, (a[0] + 1) * HALF)
+                nc.vector.quantize_mx(out=xq[:, a[1], s].bitcast(E4M3), scales=xs[:, a[1], s], in_=held["Ix", a[0], a[1]][:])
+                give(("Ix",) + a)
+            elif kind == "Qg":
+                s = slice(a[0] * CHUNK, (a[0] + 1) * CHUNK)
+                nc.vector.quantize_mx(out=gq[:, a[1], s].bitcast(E5M2), scales=gs[:, a[1], s], in_=held["Ig", a[0], a[1]][:])
+                give(("Ig",) + a)
+            elif kind == "Qw":
+                s = slice(a[1] * HALF, (a[1] + 1) * HALF)
+                nc.vector.quantize_mx(out=wq[:, a[0], s].bitcast(E4M3), scales=ws[:, a[0], s], in_=held["Iw", a[0], a[1]][:])
+                give(("Iw",) + a)
+            elif kind == "Qt":
+                s = slice(a[1] * 512, (a[1] + 1) * 512)
+                nc.vector.quantize_mx(out=gtq[:, a[0], s].bitcast(E5M2), scales=gts[:, a[0], s], in_=held["gt", a[0], a[1]][:])
+                give(("gt",) + a)
+            elif kind == "T":
+                banks = [take("bank", ("Tb",) + a + (pair,), [P, 512], F32) for pair in range(2)]
+                for j in range(PACK):
+                    words = g_raw(*a)[:, j, :].bitcast(F32)
+                    for u in range(2):
+                        o = (2 * (j % 2) + u) * P
+                        nc.tensor.transpose(banks[j // 2][:, o:o + P], words[:, u:256:2], ident[:])
+            elif kind == "C":
+                if ("gt",) + a[:2] not in held:
+                    take("gt", ("gt",) + a[:2], [P, 2048], BF16)
+                t = held["gt", a[0], a[1]]
+                dst = t[:, a[2] * 1024:(a[2] + 1) * 1024].bitcast(F32).rearrange("p (b r u) -> p b r u", b=2, u=2)
+                copy_on(engine, dst, held[("Tb",) + a][:].rearrange("p (b u r) -> p b r u", b=2, u=2))
+                give(("Tb",) + a)
+            elif kind == "W":
+                acc = held["M1", a[0], 0]
+                for i in range(a[1]):
+                    nc.tensor.matmul(acc[:], lhsT=ones[:], rhs=warm[:], start=True, stop=True)
+            elif kind == "S":
+                acc = take("bank", item, [P, 512], F32)
+                nc.tensor.matmul(acc[:, 0:P], lhsT=ones[:], rhs=srow[:], start=True, stop=True)
+            elif kind == "sc":
+                copy_on(engine, sc[:], held[("S",)][:, 0:P])
+                give(("S",))
+                for q in range(4):
+                    r = slice(32 * q, 32 * q + 32)
+                    nc.gpsimd.tensor_copy(out=sw[r, :, :], in_=sc[r, :].rearrange("p (g q k) -> p g q k", g=4, q=4)[:, :, q, :])
+            elif kind == "D":
+                if ("D",) not in held:
+                    held[("D",)] = psum.tile([P, 512], F32, name="bank" + str(BANKS - 1))
+                for i in range(a[0]):
+                    nc.tensor.matmul(held[("D",)][:], lhsT=ones[:], rhs=warm[:], start=True, stop=True)
+            elif kind == "M1":
+                nb, h, g = a
+                if g == 0:
+                    take("bank", ("M1", nb, h), [P, 512], F32)
+                n_s = slice(nb * P, (nb + 1) * P)
+                k_s = slice(h * HALF, (h + 1) * HALF)
+                nc.tensor.matmul_mx(out=held["M1", nb, h][:], lhsT=gq[:, g, n_s].bitcast(E5M2), lhsT_scale=gs[:, g, n_s],
+                                    rhs=xq[:, g, k_s].bitcast(E4M3), rhs_scale=xs[:, g, k_s],
+                                    start=(g == 0), stop=(g == 1))
+            elif kind == "E1":
+                nb, h = a
+                acc = held["M1", nb, h]
+                if ("o", nb) not in held:
+                    take("out", ("o", nb), [P, 1024], F32)
+                o = held["o", nb]
+                if engine == "v":
+                    b0 = nb * 8 + 4 * h
+                    nc.vector.tensor_tensor(
+                        out=o[:, h * HALF:(h + 1) * HALF].rearrange("p (b k) -> p b k", b=4),
+                        in0=acc[:].rearrange("p (b k) -> p b k", b=4),
+                        in1=sc[:, b0:b0 + 4].unsqueeze(2).to_broadcast([P, 4, P]), op=MULT)
+                else:
+                    for b in range(4):
+                        kb = 4 * h + b
+                        nc.scalar.activation(out=o[:, kb * P:(kb + 1) * P], in_=acc[:, b * P:(b + 1) * P], func=COPY,
+                                             scale=sc[:, nb * 8 + kb:nb * 8 + kb + 1])
+                give(("M1", nb, h))
+                if ("E1", nb, 1 - h) in done:
+                    nc.sync.dma_start(out=out_1[nb * P:(nb + 1) * P, :], in_=o[:])
+                    give(("o", nb))
+            elif kind == "M0":
+                c, tb, h = a
+                if c == 0:
+                    take("bank", ("M0", tb, h), [P, 512], F32)
+                t_s = slice(tb * P, (tb + 1) * P)
+                k_s = slice(h * HALF, (h + 1) * HALF)
+                nc.tensor.matmul_mx(out=held["M0", tb, h][:], lhsT=gtq[:, c, t_s].bitcast(E5M2), lhsT_scale=gts[:, c, t_s],
+                                    rhs=wq[:, c, k_s].bitcast(E4M3), rhs_scale=ws[:, c, k_s],
+                                    start=(c == 0), stop=(c == 3))
             else:
-                vtasks = [(iw, 0, 0, "v"), (iw, 1, 0, "v"), None, (qw, 0, 0), None, (iw, 2, 0, "v"), None, (qw, 1, 0)]
-            for i in range(8):
-                nb = 4 * c + i // 2
-                h = i % 2
-                acc = bank()
-                for g in range(2):
-                    mx1(acc, nb, h, g)
-                if vtasks[i]:
-                    vtasks[i][0](*vtasks[i][1:])
-                e1(acc, nb, h, "v" if i in V_EVAC else "s")
-                if h == 1:
-                    store1(nb)
+                tb, h = a
+                o = take("out", ("o0", tb, h), [P, 512], F32)
+                copy_on(engine, o[:], held["M0", tb, h][:])
+                give(("M0", tb, h))
+                nc.sync.dma_start(out=o0_v[tb // 4][tb % 4][:, h * HALF:(h + 1) * HALF], in_=o[:])
+                give(("o0", tb, h))
+            done.add(item)
 
-        vtasks = [[(iw, 0, 1, "v"), (qw, 2, 0)], [(iw, 1, 1, "v"), (qw, 3, 0)], [(iw, 2, 1, "v"), (qw, 0, 1)],
-                  [(qw, 1, 1)]]
-        accs = [bank() for tb in range(8)]
-        iw(3, 0, "s")
-        for c in range(4):
-            for tb in range(8):
-                mx0(accs[tb], tb, 0, c)
-            for task in vtasks[c]:
-                task[0](*task[1:])
-        for tb in range(8):
-            e0(accs[tb], tb, 0, "v" if tb % 2 else "s")
-            if tb == 1:
-                iw(3, 1, "v")
-            if tb == 3:
-                qw(2, 1)
-            if tb == 5:
-                qw(3, 1)
-        accs = [bank() for tb in range(4)]
-        for c in range(4):
-            for tb in range(4):
-                mx0(accs[tb], tb, 1, c)
-        for tb in range(4):
-            e0(accs[tb], tb, 1, "v" if tb % 2 else "s")
-        for tb in range(4, 8):
-            acc = bank()
-            for c in range(4):
-                mx0(acc, tb, 1, c)
-            e0(acc, tb, 1, "v" if tb % 2 else "s")
+        queues = {"s": items(S_SEQ), "v": items(V_SEQ), "p": items(PE_SEQ)}
+        at = {"s": 0, "v": 0, "p": 0}
+        total = sum([len(q) for q in queues.values()])
+        for turn in range(3 * total):
+            for e in ("v", "s", "p"):
+                while at[e] < len(queues[e]):
+                    item = queues[e][at[e]]
+                    if not all([n in done for n in needs(item)]) or not has_slots(item):
+                        break
+                    step(item, e)
+                    at[e] += 1
+                    if e == "p":
+                        break
+        assert sum([at[e] for e in at]) == total

@@ -45,23 +45,23 @@ PE_SEQ = (
     "M0 1 7 1, M0 2 7 1, M0 3 7 1",
 )
 V_SEQ = (
-    "Ig 0 0, Ix 0 0, Qg 0 0, Qx 0 0, Ig 0 1, sc, Qx 0 1, Qg 0 1",
-    "Ix 1 1, Qx 1 0, Qx 1 1, Ig 1 0, Ig 1 1, E1 0 1, Qg 1 1, Qt 0 0",
-    "Qg 1 0, Qt 1 0, Ig 3 0, Ig 2 1, Ig 2 0, E1 6 0, Qg 3 0, Qg 2 0",
-    "Qg 2 1, E1 7 1, Iw 1 0, Iw 0 0, Ig 3 1, Qw 0 0, Qg 3 1, Qt 2 0",
-    "C 3 1 1, E1 11 1, E1 1 1, E1 12 0, Iw 2 0, E1 14 0, Qt 0 1, E1 13 1",
-    "E1 14 1, Qw 1 0, Qw 2 0, Qt 1 1, Qt 3 1, Qt 2 1, Qt 3 0, Iw 1 1",
-    "Qw 3 0, Qw 1 1, Qw 0 1, E0 0 0, E0 1 0, E0 4 0, Qw 2 1, Iw 3 1",
+    "Ig 0 0, Ix 0 0, Qg 0 0, Qx 0 0, Qt 0 0, Ig 0 1, Qx 0 1, sc",
+    "Qg 0 1, Ix 1 1, Qx 1 0, Qx 1 1, E1 2 0, Ig 1 1, Ig 1 0, Qg 1 1",
+    "Qg 1 0, E1 2 1, Ig 2 0, Ig 2 1, E1 4 1, E1 5 1, Qg 2 1, Ig 3 1",
+    "Qg 2 0, Iw 0 0, Ig 3 0, Qt 1 0, Qg 3 0, E1 9 1, Qg 3 1, Qt 1 1",
+    "Qt 2 1, Iw 1 0, E1 11 0, E1 11 1, Qw 0 0, E1 13 0, Qw 1 0, Qt 0 1",
+    "E1 15 0, E1 15 1, E1 14 0, Iw 2 0, Qt 2 0, Qw 2 0, Qt 3 0, Qw 3 0",
+    "Iw 1 1, Qw 0 1, Qt 3 1, E0 0 0, E0 4 0, Qw 1 1, Qw 2 1, Iw 3 1",
     "Qw 3 1",
 )
 S_SEQ = (
-    "C 0 0 1, C 0 0 0, Ix 0 1, Ix 1 0, E1 1 0, C 0 1 1, E1 0 0, C 1 0 1",
-    "E1 2 0, C 1 1 0, E1 3 0, C 1 0 0, C 0 1 0, C 2 0 0, C 1 1 1, E1 3 1",
-    "E1 4 1, C 2 0 1, E1 4 0, E1 5 0, C 2 1 0, E1 2 1, E1 7 0, C 2 1 1",
-    "E1 5 1, E1 8 0, C 3 0 0, E1 6 1, E1 8 1, C 3 0 1, E1 9 0, E1 9 1",
-    "E1 10 0, C 3 1 0, E1 11 0, E1 12 1, E1 10 1, E1 13 0, E1 15 0, E1 15 1",
-    "Iw 3 0, Iw 0 1, Iw 2 1, E0 7 0, E0 6 0, E0 3 0, E0 5 0, E0 0 1",
-    "E0 3 1, E0 1 1, E0 2 0, E0 2 1, E0 5 1, E0 4 1, E0 6 1, E0 7 1",
+    "C 0 0 1, C 0 0 0, Ix 0 1, Ix 1 0, E1 0 0, E1 3 0, E1 1 0, C 1 0 0",
+    "E1 1 1, E1 0 1, C 1 0 1, C 0 1 1, C 1 1 1, C 0 1 0, E1 3 1, E1 4 0",
+    "C 2 0 0, E1 5 0, C 1 1 0, C 2 0 1, E1 6 0, C 2 1 1, C 2 1 0, E1 7 1",
+    "E1 7 0, E1 8 0, E1 6 1, E1 9 0, E1 8 1, C 3 0 0, E1 10 0, C 3 0 1",
+    "C 3 1 1, C 3 1 0, E1 12 0, E1 10 1, E1 12 1, E1 14 1, E1 13 1, Iw 3 0",
+    "Iw 0 1, Iw 2 1, E0 1 0, E0 5 0, E0 7 0, E0 3 0, E0 2 0, E0 6 0",
+    "E0 1 1, E0 2 1, E0 3 1, E0 0 1, E0 5 1, E0 4 1, E0 6 1, E0 7 1",
 )
 
 
@@ -86,13 +86,13 @@ def tile_fp8columnparallellinear_v_kernel(tc, x, weight, weight_scale_inv, bias,
         psum = ctx.enter_context(tc.psum_pool(name="psum", bufs=1))
         ctx.enter_context(tc.manual_schedule())
 
-        def tile(name, shape, dtype):
-            return sbuf.tile(shape, dtype, name=name, align_bytes=64)
+        def tile(name, shape, dtype, align=64):
+            return sbuf.tile(shape, dtype, name=name, align_bytes=align)
 
-        xq, xs = tile("xq", [P, 2, K], U32), tile("xs", [P, 2, K], U8)
-        gq, gs = tile("gq", [P, 2, N], U32), tile("gs", [P, 2, N], U8)
-        gtq, gts = tile("gtq", [P, 4, TOKENS], U32), tile("gts", [P, 4, TOKENS], U8)
-        wq, ws = tile("wq", [P, 4, K], U32), tile("ws", [P, 4, K], U8)
+        xq, xs = tile("xq", [P, 2, K], U32, 256), tile("xs", [P, 2, K], U8, 256)
+        gq, gs = tile("gq", [P, 2, N], U32, 256), tile("gs", [P, 2, N], U8, 256)
+        gtq, gts = tile("gtq", [P, 4, TOKENS], U32, 256), tile("gts", [P, 4, TOKENS], U8, 256)
+        wq, ws = tile("wq", [P, 4, K], U32, 256), tile("ws", [P, 4, K], U8, 256)
         ident = tile("ident", [P, P], F32)
         ones = tile("ones", [P, P], BF16)
         warm = tile("warm", [P, 512], BF16)

from contextlib import ExitStack

import concourse.mybir as mybir
from concourse.masks import make_identity

TOKENS, K, N = 1024, 1024, 2048
FLOPS = 2 * 2 * TOKENS * K * N
BYTES = 2 * (TOKENS * K + N * K + 16 * 8 + TOKENS * N) + 4 * (TOKENS * K + N * K)

F32 = mybir.dt.float32
BF16 = mybir.dt.bfloat16
U32 = mybir.dt.uint32
U8 = mybir.dt.uint8
E4M3 = mybir.dt.float8_e4m3fn_x4
E5M2 = mybir.dt.float8_e5m2_x4
COPY = mybir.ActivationFunctionType.Copy
MULT = mybir.AluOpType.mult

P = 128
PACK = 4
HALF = 512
CHUNK = 512
BANKS = 8
IN_BUFS, GT_BUFS, OUT_BUFS = 6, 8, 10
LOADS = ("g 0 1 0", "x 0 1 0", "s 0", "x 0 1 1", "g 0 1 1", "x 1 1 0", "x 1 1 1", "g 1 1 0", "g 1 1 1", "g 2 2 0", "g 2 2 1", "w 0", "w 1",)

PE_SEQ = (
    "D 4, T 0 0, D 6, M1 0 0 0, M1 1 0 0, M1 2 0 0, M1 3 0 0, S",
    "T 0 1, M1 0 0 1, M1 1 0 1, M1 2 0 1, M1 3 0 1, T 1 0, M1 0 1 0, M1 0 1 1",
    "M1 1 1 0, M1 1 1 1, T 1 1, M1 2 1 0, M1 2 1 1, M1 3 1 0, M1 3 1 1, T 2 0",
    "M1 4 0 0, M1 4 0 1, M1 4 1 0, M1 4 1 1, M1 5 0 0, M1 5 0 1, M1 5 1 0, M1 5 1 1",
    "T 2 1, M1 6 0 0, M1 6 0 1, M1 6 1 0, M1 6 1 1, M1 7 0 0, M1 7 0 1, M1 7 1 0",
    "M1 7 1 1, T 3 0, M1 8 0 0, M1 8 0 1, M1 8 1 0, M1 8 1 1, M1 9 0 0, M1 9 0 1",
    "M1 9 1 0, M1 9 1 1, T 3 1, M1 10 0 0, M1 10 0 1, M1 10 1 0, M1 10 1 1, M1 11 0 0",
    "M1 11 0 1, M1 11 1 0, M1 11 1 1, M1 12 0 0, M1 12 0 1, M1 12 1 0, M1 12 1 1, M1 13 0 0",
    "M1 13 0 1, M1 13 1 0, M1 13 1 1, M1 14 0 0, M1 14 0 1, M1 14 1 0, M1 14 1 1, M1 15 0 0",
    "M1 15 0 1, M1 15 1 0, M1 15 1 1, M0 0 0 0, M0 0 1 0, M0 0 2 0, M0 0 3 0, M0 0 4 0",
    "M0 0 5 0, M0 0 6 0, M0 0 7 0, M0 1 0 0, M0 1 1 0, M0 1 2 0, M0 1 3 0, M0 1 4 0",
    "M0 1 5 0, M0 1 6 0, M0 1 7 0, M0 2 0 0, M0 2 1 0, M0 2 2 0, M0 2 3 0, M0 2 4 0",
    "M0 2 5 0, M0 2 6 0, M0 2 7 0, M0 3 0 0, M0 3 1 0, M0 3 2 0, M0 3 3 0, M0 3 4 0",
    "M0 3 5 0, M0 3 6 0, M0 3 7 0, M0 0 0 1, M0 0 1 1, M0 0 2 1, M0 0 3 1, M0 1 0 1",
    "M0 1 1 1, M0 1 2 1, M0 1 3 1, M0 2 0 1, M0 2 1 1, M0 2 2 1, M0 2 3 1, M0 3 0 1",
    "M0 3 1 1, M0 3 2 1, M0 3 3 1, M0 0 4 1, M0 1 4 1, M0 2 4 1, M0 3 4 1, M0 0 5 1",
    "M0 1 5 1, M0 2 5 1, M0 3 5 1, M0 0 6 1, M0 1 6 1, M0 2 6 1, M0 3 6 1, M0 0 7 1",
    "M0 1 7 1, M0 2 7 1, M0 3 7 1",
)
V_SEQ = (
    "Ig 0 0, Ix 0 0, Qg 0 0, Qx 0 0, Qt 0 0, Ig 0 1, Qx 0 1, sc",
    "Qg 0 1, Ix 1 1, Qx 1 0, Qx 1 1, E1 2 0, Ig 1 1, Ig 1 0, Qg 1 1",
    "Qg 1 0, E1 2 1, Ig 2 0, Ig 2 1, E1 4 1, E1 5 1, Qg 2 1, Ig 3 1",
    "Qg 2 0, Iw 0 0, Ig 3 0, Qt 1 0, Qg 3 0, E1 9 1, Qg 3 1, Qt 1 1",
    "Qt 2 1, Iw 1 0, E1 11 0, E1 11 1, Qw 0 0, E1 13 0, Qw 1 0, Qt 0 1",
    "E1 15 0, E1 15 1, E1 14 0, Iw 2 0, Qt 2 0, Qw 2 0, Qt 3 0, Qw 3 0",
    "Iw 1 1, Qw 0 1, Qt 3 1, E0 0 0, E0 4 0, Qw 1 1, Qw 2 1, Iw 3 1",
    "Qw 3 1",
)
S_SEQ = (
    "C 0 0 1, C 0 0 0, Ix 0 1, Ix 1 0, E1 0 0, E1 3 0, E1 1 0, C 1 0 0",
    "E1 1 1, E1 0 1, C 1 0 1, C 0 1 1, C 1 1 1, C 0 1 0, E1 3 1, E1 4 0",
    "C 2 0 0, E1 5 0, C 1 1 0, C 2 0 1, E1 6 0, C 2 1 1, C 2 1 0, E1 7 1",
    "E1 7 0, E1 8 0, E1 6 1, E1 9 0, E1 8 1, C 3 0 0, E1 10 0, C 3 0 1",
    "C 3 1 1, C 3 1 0, E1 12 0, E1 10 1, E1 12 1, E1 14 1, E1 13 1, Iw 3 0",
    "Iw 0 1, Iw 2 1, E0 1 0, E0 5 0, E0 7 0, E0 3 0, E0 2 0, E0 6 0",
    "E0 1 1, E0 2 1, E0 3 1, E0 0 1, E0 5 1, E0 4 1, E0 6 1, E0 7 1",
)


def parse(text):
    words = text.split(" ")
    return tuple([words[0]] + [int(w) for w in words[1:]])


def items(lines):
    return [parse(t) for line in lines for t in line.split(", ")]


def tile_fp8columnparallellinear_v_kernel(tc, x, weight, weight_scale_inv, bias, grad_out, out_0, out_1):
    nc = tc.nc
    x_v = x.rearrange("(g p j) k -> g p j k", p=P, j=PACK)
    g_v = grad_out.rearrange("(g p j) n -> g p j n", p=P, j=PACK)
    w_v = weight.rearrange("(g p j) k -> g p j k", p=P, j=PACK)
    o0_v = out_0.rearrange("(g p j) k -> g j p k", p=P, j=PACK)

    with ExitStack() as ctx:
        sbuf = ctx.enter_context(tc.tile_pool(name="sbuf", bufs=1))
        psum = ctx.enter_context(tc.psum_pool(name="psum", bufs=1))
        ctx.enter_context(tc.manual_schedule())

        def tile(name, shape, dtype, align=64):
            return sbuf.tile(shape, dtype, name=name, align_bytes=align)

        xq, xs = tile("xq", [P, 2, K], U32, 256), tile("xs", [P, 2, K], U8, 256)
        gq, gs = tile("gq", [P, 2, N], U32, 256), tile("gs", [P, 2, N], U8, 256)
        gtq, gts = tile("gtq", [P, 4, TOKENS], U32, 256), tile("gts", [P, 4, TOKENS], U8, 256)
        wq, ws = tile("wq", [P, 4, K], U32, 256), tile("ws", [P, 4, K], U8, 256)
        ident = tile("ident", [P, P], F32)
        ones = tile("ones", [P, P], BF16)
        warm = tile("warm", [P, 512], BF16)
        srow = tile("srow", [P, P], BF16)
        sc = tile("sc", [P, P], F32)
        sw = tile("sw", [P, 4, 8], F32)
        dummy = tile("dummy", [P, 1], F32)

        x_pair = [tile("x_or_w%d" % h, [P, 2, PACK, HALF], BF16) for h in range(2)]
        g_tiles = {}
        w_raw = {g: tile("w_raw%d" % g, [P, PACK, K], BF16) for g in range(2)}

        def x_raw(h, g):
            return x_pair[h][:, g, :, :]

        def g_raw(c, g):
            t, first = g_tiles[c, g]
            return t[:, :, (c - first) * CHUNK:(c - first + 1) * CHUNK]

        nc.vector.memset(ones[:], 1.0)
        nc.vector.memset(warm[:], 0.0)
        nc.vector.memset(srow[:], 0.0)
        nc.vector.memset(dummy[:], 0.0)
        nc.scalar.activation(out=dummy[:], in_=dummy[:], func=COPY)
        make_identity(nc, ident[:])

        for load in items(LOADS):
            kind, a = load[0], load[1]
            if kind == "x":
                nc.sync.dma_start(out=x_raw(a, load[3]), in_=x_v[load[3]][:, :, a * HALF:(a + 1) * HALF])
            elif kind == "g":
                t = tile("g_raw%d%d" % (a, load[3]), [P, PACK, load[2] * CHUNK], BF16)
                for c in range(a, a + load[2]):
                    g_tiles[c, load[3]] = (t, a)
                nc.sync.dma_start(out=t[:], in_=g_v[load[3]][:, :, a * CHUNK:(a + load[2]) * CHUNK])
            elif kind == "s":
                nc.sync.dma_start(out=srow[0:1, :], in_=weight_scale_inv.rearrange("(o a) b -> o (a b)", o=1))
            else:
                nc.sync.dma_start(out=w_raw[a][:], in_=w_v[a])

        free = {"in": list(range(IN_BUFS)), "gt": list(range(GT_BUFS)), "out": list(range(OUT_BUFS)), "bank": list(range(BANKS))}
        slot_of = {}
        held = {}
        done = set()

        def take(kind, key, shape, dtype):
            slot = free[kind][0]
            free[kind].remove(slot)
            slot_of[key] = (kind, slot)
            name = kind + str(slot)
            if kind == "bank":
                held[key] = psum.tile(shape, dtype, name=name)
            else:
                held[key] = tile(name, shape, dtype)
            return held[key]

        def give(key):
            kind, slot = slot_of[key]
            free[kind].append(slot)

        def lay(t):
            return t.rearrange("p (c i t) -> p c t i", i=4, t=PACK)

        def cols(src):
            return src.rearrange("p t (c i) -> p c t i", i=4)

        def copy_on(engine, out, src):
            if engine == "v":
                nc.vector.tensor_copy(out=out, in_=src)
            else:
                nc.scalar.copy(out=out, in_=src)

        def needs(item):
            kind = item[0]
            a = item[1:]
            if kind == "Iw":
                return [("sc",)] + ([("Ix", a[0] - 2, 0), ("Ix", a[0] - 2, 1)] if a[0] > 1 else [])
            if kind in ("Qx", "Qg", "Qw"):
                return [("I" + kind[1],) + a]
            if kind == "sc":
                return [("S",)]
            if kind == "C":
                return [("T",) + a[:2]]
            if kind == "Qt":
                return [("C",) + a + (0,), ("C",) + a + (1,)]
            if kind == "E1":
                return [("M1",) + a + (1,), ("sc",)]
            if kind == "E0":
                return [("M0", 3) + a]
            if kind == "M1":
                return [("Qg", a[0] // 4, a[2]), ("Qx", a[1], a[2])]
            if kind == "M0":
                return [("Qw", a[0], a[2]), ("Qt", a[0], a[1] // 4)]
            return []

        def has_slots(item):
            kind = item[0]
            if kind in ("Ix", "Ig", "Iw"):
                return len(free["in"]) > 0
            if kind == "C":
                return ("gt",) + item[1:3] in held or len(free["gt"]) > 0
            if kind == "E1":
                return ("o",) + item[1:2] in held or len(free["out"]) > 0
            if kind == "E0":
                return len(free["out"]) > 0
            if kind == "T":
                return len(free["bank"]) > 1
            if kind == "S" or (kind == "M1" and item[3] == 0) or (kind == "M0" and item[1] == 0):
                return len(free["bank"]) > 0
            return True

        def step(item, engine):
            kind = item[0]
            a = item[1:]
            if kind in ("Ix", "Ig"):
                t = take("in", item, [P, 2048], BF16)
                copy_on(engine, lay(t[:]), cols(x_raw(*a) if kind == "Ix" else g_raw(*a)))
                if kind == "Ix" and ("Ix", a[0], 1 - a[1]) in done:
                    w_raw[2 + a[0]] = tile("x_or_w%d" % a[0], [P, PACK, K], BF16)
                    nc.sync.dma_start(out=w_raw[2 + a[0]][:], in_=w_v[2 + a[0]])
            elif kind == "Iw":
                t = take("in", item, [P, 2048], BF16)
                g, h = a
                for b in range(4):
                    kb = 4 * h + b
                    dst = lay(t[:, b * 512:(b + 1) * 512])
                    src = cols(w_raw[g][:, :, kb * P:(kb + 1) * P])
                    if engine == "v":
                        nc.vector.tensor_scalar(out=dst, in0=src, scalar1=sw[:, g, kb:kb + 1], scalar2=None, op0=MULT)
                    else:
                        nc.scalar.activation(out=dst, in_=src, func=COPY, scale=sw[:, g, kb:kb + 1])
            elif kind == "Qx":
                s = slice(a[0] * HALF, (a[0] + 1) * HALF)
                nc.vector.quantize_mx(out=xq[:, a[1], s].bitcast(E4M3), scales=xs[:, a[1], s], in_=held["Ix", a[0], a[1]][:])
                give(("Ix",) + a)
            elif kind == "Qg":
                s = slice(a[0] * CHUNK, (a[0] + 1) * CHUNK)
                nc.vector.quantize_mx(out=gq[:, a[1], s].bitcast(E5M2), scales=gs[:, a[1], s], in_=held["Ig", a[0], a[1]][:])
                give(("Ig",) + a)
            elif kind == "Qw":
                s = slice(a[1] * HALF, (a[1] + 1) * HALF)
                nc.vector.quantize_mx(out=wq[:, a[0], s].bitcast(E4M3), scales=ws[:, a[0], s], in_=held["Iw", a[0], a[1]][:])
                give(("Iw",) + a)
            elif kind == "Qt":
                s = slice(a[1] * 512, (a[1] + 1) * 512)
                nc.vector.quantize_mx(out=gtq[:, a[0], s].bitcast(E5M2), scales=gts[:, a[0], s], in_=held["gt", a[0], a[1]][:])
                give(("gt",) + a)
            elif kind == "T":
                banks = [take("bank", ("Tb",) + a + (pair,), [P, 512], F32) for pair in range(2)]
                for j in range(PACK):
                    words = g_raw(*a)[:, j, :].bitcast(F32)
                    for u in range(2):
                        o = (2 * (j % 2) + u) * P
                        nc.tensor.transpose(banks[j // 2][:, o:o + P], words[:, u:256:2], ident[:])
            elif kind == "C":
                if ("gt",) + a[:2] not in held:
                    take("gt", ("gt",) + a[:2], [P, 2048], BF16)
                t = held["gt", a[0], a[1]]
                dst = t[:, a[2] * 1024:(a[2] + 1) * 1024].bitcast(F32).rearrange("p (b r u) -> p b r u", b=2, u=2)
                copy_on(engine, dst, held[("Tb",) + a][:].rearrange("p (b u r) -> p b r u", b=2, u=2))
                give(("Tb",) + a)
            elif kind == "W":
                acc = held["M1", a[0], 0]
                for i in range(a[1]):
                    nc.tensor.matmul(acc[:], lhsT=ones[:], rhs=warm[:], start=True, stop=True)
            elif kind == "S":
                acc = take("bank", item, [P, 512], F32)
                nc.tensor.matmul(acc[:, 0:P], lhsT=ones[:], rhs=srow[:], start=True, stop=True)
            elif kind == "sc":
                copy_on(engine, sc[:], held[("S",)][:, 0:P])
                give(("S",))
                for q in range(4):
                    r = slice(32 * q, 32 * q + 32)
                    nc.gpsimd.tensor_copy(out=sw[r, :, :], in_=sc[r, :].rearrange("p (g q k) -> p g q k", g=4, q=4)[:, :, q, :])
            elif kind == "D":
                if ("D",) not in held:
                    held[("D",)] = psum.tile([P, 512], F32, name="bank" + str(BANKS - 1))
                for i in range(a[0]):
                    nc.tensor.matmul(held[("D",)][:], lhsT=ones[:], rhs=warm[:], start=True, stop=True)
            elif kind == "M1":
                nb, h, g = a
                if g == 0:
                    take("bank", ("M1", nb, h), [P, 512], F32)
                n_s = slice(nb * P, (nb + 1) * P)
                k_s = slice(h * HALF, (h + 1) * HALF)
                nc.tensor.matmul_mx(out=held["M1", nb, h][:], lhsT=gq[:, g, n_s].bitcast(E5M2), lhsT_scale=gs[:, g, n_s],
                                    rhs=xq[:, g, k_s].bitcast(E4M3), rhs_scale=xs[:, g, k_s],
                                    start=(g == 0), stop=(g == 1))
            elif kind == "E1":
                nb, h = a
                acc = held["M1", nb, h]
                if ("o", nb) not in held:
                    take("out", ("o", nb), [P, 1024], F32)
                o = held["o", nb]
                if engine == "v":
                    b0 = nb * 8 + 4 * h
                    nc.vector.tensor_tensor(
                        out=o[:, h * HALF:(h + 1) * HALF].rearrange("p (b k) -> p b k", b=4),
                        in0=acc[:].rearrange("p (b k) -> p b k", b=4),
                        in1=sc[:, b0:b0 + 4].unsqueeze(2).to_broadcast([P, 4, P]), op=MULT)
                else:
                    for b in range(4):
                        kb = 4 * h + b
                        nc.scalar.activation(out=o[:, kb * P:(kb + 1) * P], in_=acc[:, b * P:(b + 1) * P], func=COPY,
                                             scale=sc[:, nb * 8 + kb:nb * 8 + kb + 1])
                give(("M1", nb, h))
                if ("E1", nb, 1 - h) in done:
                    nc.sync.dma_start(out=out_1[nb * P:(nb + 1) * P, :], in_=o[:])
                    give(("o", nb))
            elif kind == "M0":
                c, tb, h = a
                if c == 0:
                    take("bank", ("M0", tb, h), [P, 512], F32)
                t_s = slice(tb * P, (tb + 1) * P)
                k_s = slice(h * HALF, (h + 1) * HALF)
                nc.tensor.matmul_mx(out=held["M0", tb, h][:], lhsT=gtq[:, c, t_s].bitcast(E5M2), lhsT_scale=gts[:, c, t_s],
                                    rhs=wq[:, c, k_s].bitcast(E4M3), rhs_scale=ws[:, c, k_s],
                                    start=(c == 0), stop=(c == 3))
            else:
                tb, h = a
                o = take("out", ("o0", tb, h), [P, 512], F32)
                copy_on(engine, o[:], held["M0", tb, h][:])
                give(("M0", tb, h))
                nc.sync.dma_start(out=o0_v[tb // 4][tb % 4][:, h * HALF:(h + 1) * HALF], in_=o[:])
                give(("o0", tb, h))
            done.add(item)

        queues = {"s": items(S_SEQ), "v": items(V_SEQ), "p": items(PE_SEQ)}
        at = {"s": 0, "v": 0, "p": 0}
        total = sum([len(q) for q in queues.values()])
        for turn in range(3 * total):
            for e in ("v", "s", "p"):
                while at[e] < len(queues[e]):
                    item = queues[e][at[e]]
                    if not all([n in done for n in needs(item)]) or not has_slots(item):
                        break
                    step(item, e)
                    at[e] += 1
                    if e == "p":
                        break
        assert sum([at[e] for e in at]) == total
